import numpy as np
import ml_dtypes

BF16 = ml_dtypes.bfloat16


def bf(x):
    return np.asarray(x, np.float32).astype(BF16)


def f32(x):
    return np.asarray(x, np.float32)


def f64(x):
    return np.asarray(x).astype(np.float64)


def striped(idx):
    return np.tile(idx.reshape(-1, 16).T, (8, 1))


D, S, M, N = 128, 2048, 512, 512


def setup_inputs():
    return {"table": bf(np.random.standard_normal((D, S))), "w": bf(np.random.standard_normal((D, M))), "offs": striped(np.random.permutation(np.tile(np.arange(S), 2))[:N])}


def reference(table, w, offs):
    idx = offs[:16].T.reshape(-1)
    norm = np.sqrt(np.sum(f64(w) ** 2, axis=0))[:, None]
    return (f64(w).T @ f64(table)[:, idx]) / norm

@@ -1,0 +1,52 @@
+import concourse.mybir as mybir
+
+P = 128
+S, M, N = 2048, 512, 512
+BLOCKS = M // P
+FLOPS = 2 * P * M * N
+
+BF16, F32, U16 = mybir.dt.bfloat16, mybir.dt.float32, mybir.dt.uint16
+MULT = mybir.AluOpType.mult
+
+
+def tile_clustermemory_kernel(tc, table, w, offs, out):
+    nc = tc.nc
+    with (
+        tc.tile_pool(name="held", bufs=1) as held,
+        tc.tile_pool(name="staging", bufs=BLOCKS) as staging,
+        tc.psum_pool(name="sums", bufs=1) as sums,
+        tc.psum_pool(name="products", bufs=BLOCKS) as products,
+    ):
+        offsets = held.tile([P, N // 16], U16, name="offsets")
+        nc.sync.dma_start(offsets[:], offs)
+        samples = held.tile([P, M], BF16, name="samples")
+        nc.sync.dma_start(samples[:], w)
+        bank = held.tile([P, S], BF16, name="bank")
+        nc.sync.dma_start(bank[:], table)
+
+        ones = held.tile([P, 1], F32, name="ones")
+        nc.vector.memset(ones[:], 1.0)
+        squares = held.tile([P, M], F32, name="squares")
+        nc.vector.tensor_tensor(squares[:], samples[:], samples[:], MULT)
+        square_sums = sums.tile([P, BLOCKS], F32, name="square_sums")
+        for b in range(BLOCKS):
+            nc.tensor.matmul(
+                square_sums[:, b : b + 1], squares[:, b * P : (b + 1) * P], ones[:],
+                start=True, stop=True,
+            )
+        norms = held.tile([P, BLOCKS], F32, name="norms")
+        nc.scalar.sqrt(norms[:], square_sums[:])
+        inverse_norms = held.tile([P, BLOCKS], F32, name="inverse_norms")
+        nc.vector.reciprocal(inverse_norms[:], norms[:])
+
+        for b in range(BLOCKS):
+            product = products.tile([P, N], F32, name="product")
+            nc.tensor.matmul(
+                product[:], samples[:, b * P : (b + 1) * P], bank[:].indirect(offsets[:]),
+                start=True, stop=True,
+            )
+            scaled = staging.tile([P, N], F32, name="scaled")
+            nc.vector.tensor_scalar(
+                scaled[:], product[:], inverse_norms[:, b : b + 1], None, MULT
+            )
+            nc.sync.dma_start(out[b * P : (b + 1) * P, :], scaled[:])

@@ -20,14 +20,16 @@ def tile_clustermemory_kernel(tc, table, w, offs, out):
         offsets = held.tile([P, N // 16], U16, name="offsets")
         nc.sync.dma_start(offsets[:], offs)
         samples = held.tile([P, M], BF16, name="samples")
-        nc.sync.dma_start(samples[:], w)
+        nc.scalar.dma_start(samples[:], w)
         bank = held.tile([P, S], BF16, name="bank")
-        nc.sync.dma_start(bank[:], table)
+        for half, queue in enumerate((nc.sync, nc.scalar)):
+            columns = slice(half * (S // 2), (half + 1) * (S // 2))
+            queue.dma_start(bank[:, columns], table[:, columns])
 
         ones = held.tile([P, 1], F32, name="ones")
         nc.vector.memset(ones[:], 1.0)
         squares = held.tile([P, M], F32, name="squares")
-        nc.vector.tensor_tensor(squares[:], samples[:], samples[:], MULT)
+        nc.scalar.square(squares[:], samples[:])
         square_sums = sums.tile([P, BLOCKS], F32, name="square_sums")
         for b in range(BLOCKS):
             nc.tensor.matmul(

@@ -4,6 +4,7 @@ P = 128
 S, M, N = 2048, 512, 512
 BLOCKS = M // P
 FLOPS = 2 * P * M * N
+WARM_UP = 4
 
 BF16, F32, U16 = mybir.dt.bfloat16, mybir.dt.float32, mybir.dt.uint16
 MULT = mybir.AluOpType.mult
@@ -17,24 +18,30 @@ def tile_clustermemory_kernel(tc, table, w, offs, out):
         tc.psum_pool(name="sums", bufs=1) as sums,
         tc.psum_pool(name="products", bufs=BLOCKS) as products,
     ):
+        samples = held.tile([P, M], BF16, name="samples")
+        nc.sync.dma_start(samples[:], w)
         offsets = held.tile([P, N // 16], U16, name="offsets")
         nc.sync.dma_start(offsets[:], offs)
-        samples = held.tile([P, M], BF16, name="samples")
-        nc.scalar.dma_start(samples[:], w)
         bank = held.tile([P, S], BF16, name="bank")
-        for half, queue in enumerate((nc.sync, nc.scalar)):
+        for half, queue in enumerate((nc.scalar, nc.sync)):
             columns = slice(half * (S // 2), (half + 1) * (S // 2))
             queue.dma_start(bank[:, columns], table[:, columns])
+
+        zeros = held.tile([P, N], BF16, name="zeros")
+        nc.vector.memset(zeros[:], 0.0)
+        unused = sums.tile([P, N], F32, name="unused")
+        for i in range(WARM_UP):
+            nc.tensor.matmul(unused[:], zeros[:, :P], zeros[:], start=True, stop=True)
 
         ones = held.tile([P, 1], F32, name="ones")
         nc.vector.memset(ones[:], 1.0)
         squares = held.tile([P, M], F32, name="squares")
-        nc.scalar.square(squares[:], samples[:])
         square_sums = sums.tile([P, BLOCKS], F32, name="square_sums")
         for b in range(BLOCKS):
+            block = slice(b * P, (b + 1) * P)
+            nc.vector.tensor_tensor(squares[:, block], samples[:, block], samples[:, block], MULT)
             nc.tensor.matmul(
-                square_sums[:, b : b + 1], squares[:, b * P : (b + 1) * P], ones[:],
-                start=True, stop=True,
+                square_sums[:, b : b + 1], squares[:, block], ones[:], start=True, stop=True
             )
         norms = held.tile([P, BLOCKS], F32, name="norms")
         nc.scalar.sqrt(norms[:], square_sums[:])

@@ -55,7 +55,11 @@ def tile_clustermemory_kernel(tc, table, w, offs, out):
                 start=True, stop=True,
             )
             scaled = staging.tile([P, N], F32, name="scaled")
-            nc.vector.tensor_scalar(
-                scaled[:], product[:], inverse_norms[:, b : b + 1], None, MULT
-            )
-            nc.sync.dma_start(out[b * P : (b + 1) * P, :], scaled[:])
+            if b % 2 == 0:
+                nc.vector.tensor_scalar(
+                    scaled[:], product[:], inverse_norms[:, b : b + 1], None, MULT
+                )
+                nc.sync.dma_start(out[b * P : (b + 1) * P, :], scaled[:])
+            else:
+                nc.scalar.mul(scaled[:], product[:], inverse_norms[:, b : b + 1])
+                nc.scalar.dma_start(out[b * P : (b + 1) * P, :], scaled[:])

@@ -59,7 +59,6 @@ def tile_clustermemory_kernel(tc, table, w, offs, out):
                 nc.vector.tensor_scalar(
                     scaled[:], product[:], inverse_norms[:, b : b + 1], None, MULT
                 )
-                nc.sync.dma_start(out[b * P : (b + 1) * P, :], scaled[:])
             else:
                 nc.scalar.mul(scaled[:], product[:], inverse_norms[:, b : b + 1])
-                nc.scalar.dma_start(out[b * P : (b + 1) * P, :], scaled[:])
+            nc.sync.dma_start(out[b * P : (b + 1) * P, :], scaled[:])

@@ -3,7 +3,9 @@ import concourse.mybir as mybir
 P = 128
 S, M, N = 2048, 512, 512
 BLOCKS = M // P
+PER_COLUMN = 16
 FLOPS = 2 * P * M * N
+
 WARM_UP = 4
 
 BF16, F32, U16 = mybir.dt.bfloat16, mybir.dt.float32, mybir.dt.uint16
@@ -15,28 +17,28 @@ def tile_clustermemory_kernel(tc, table, w, offs, out):
     with (
         tc.tile_pool(name="held", bufs=1) as held,
         tc.tile_pool(name="staging", bufs=BLOCKS) as staging,
-        tc.psum_pool(name="sums", bufs=1) as sums,
         tc.psum_pool(name="products", bufs=BLOCKS) as products,
+        tc.psum_pool(name="others", bufs=1) as others,
     ):
         samples = held.tile([P, M], BF16, name="samples")
         nc.sync.dma_start(samples[:], w)
-        offsets = held.tile([P, N // 16], U16, name="offsets")
+        offsets = held.tile([P, N // PER_COLUMN], U16, name="offsets")
         nc.sync.dma_start(offsets[:], offs)
-        bank = held.tile([P, S], BF16, name="bank")
+        centres = held.tile([P, S], BF16, name="centres")
         for half, queue in enumerate((nc.scalar, nc.sync)):
             columns = slice(half * (S // 2), (half + 1) * (S // 2))
-            queue.dma_start(bank[:, columns], table[:, columns])
+            queue.dma_start(centres[:, columns], table[:, columns])
 
         zeros = held.tile([P, N], BF16, name="zeros")
         nc.vector.memset(zeros[:], 0.0)
-        unused = sums.tile([P, N], F32, name="unused")
+        idle_product = others.tile([P, N], F32, name="idle_product")
         for i in range(WARM_UP):
-            nc.tensor.matmul(unused[:], zeros[:, :P], zeros[:], start=True, stop=True)
+            nc.tensor.matmul(idle_product[:], zeros[:, :P], zeros[:], start=True, stop=True)
 
         ones = held.tile([P, 1], F32, name="ones")
         nc.vector.memset(ones[:], 1.0)
         squares = held.tile([P, M], F32, name="squares")
-        square_sums = sums.tile([P, BLOCKS], F32, name="square_sums")
+        square_sums = others.tile([P, BLOCKS], F32, name="square_sums")
         for b in range(BLOCKS):
             block = slice(b * P, (b + 1) * P)
             nc.vector.tensor_tensor(squares[:, block], samples[:, block], samples[:, block], MULT)
@@ -49,16 +51,14 @@ def tile_clustermemory_kernel(tc, table, w, offs, out):
         nc.vector.reciprocal(inverse_norms[:], norms[:])
 
         for b in range(BLOCKS):
+            block = slice(b * P, (b + 1) * P)
             product = products.tile([P, N], F32, name="product")
             nc.tensor.matmul(
-                product[:], samples[:, b * P : (b + 1) * P], bank[:].indirect(offsets[:]),
+                product[:], samples[:, block], centres[:].indirect(offsets[:]),
                 start=True, stop=True,
             )
             scaled = staging.tile([P, N], F32, name="scaled")
-            if b % 2 == 0:
-                nc.vector.tensor_scalar(
-                    scaled[:], product[:], inverse_norms[:, b : b + 1], None, MULT
-                )
-            else:
-                nc.scalar.mul(scaled[:], product[:], inverse_norms[:, b : b + 1])
-            nc.sync.dma_start(out[b * P : (b + 1) * P, :], scaled[:])
+            nc.vector.tensor_scalar(
+                scaled[:], product[:], inverse_norms[:, b : b + 1], None, MULT
+            )
+            nc.sync.dma_start(out[block, :], scaled[:])

@@ -1,9 +1,11 @@
 import concourse.mybir as mybir
+from concourse.masks import make_identity
 
 P = 128
 S, M, N = 2048, 512, 512
 BLOCKS = M // P
 PER_COLUMN = 16
+BANK = 512
 FLOPS = 2 * P * M * N
 
 WARM_UP = 4
@@ -18,7 +20,7 @@ def tile_clustermemory_kernel(tc, table, w, offs, out):
         tc.tile_pool(name="held", bufs=1) as held,
         tc.tile_pool(name="staging", bufs=BLOCKS) as staging,
         tc.psum_pool(name="products", bufs=BLOCKS) as products,
-        tc.psum_pool(name="others", bufs=1) as others,
+        tc.psum_pool(name="grams", bufs=BLOCKS) as grams,
     ):
         samples = held.tile([P, M], BF16, name="samples")
         nc.sync.dma_start(samples[:], w)
@@ -31,24 +33,28 @@ def tile_clustermemory_kernel(tc, table, w, offs, out):
 
         zeros = held.tile([P, N], BF16, name="zeros")
         nc.vector.memset(zeros[:], 0.0)
-        idle_product = others.tile([P, N], F32, name="idle_product")
+        idle_product = products.tile([P, N], F32, name="product")
         for i in range(WARM_UP):
             nc.tensor.matmul(idle_product[:], zeros[:, :P], zeros[:], start=True, stop=True)
 
-        ones = held.tile([P, 1], F32, name="ones")
-        nc.vector.memset(ones[:], 1.0)
-        squares = held.tile([P, M], F32, name="squares")
-        square_sums = others.tile([P, BLOCKS], F32, name="square_sums")
+        identity = held.tile([P, P], F32, name="identity")
+        make_identity(nc, identity[:])
+        diagonal = held.tile([P, P], F32, name="diagonal")
+        square_sums = held.tile([P, BLOCKS], F32, name="square_sums")
         for b in range(BLOCKS):
             block = slice(b * P, (b + 1) * P)
-            nc.vector.tensor_tensor(squares[:, block], samples[:, block], samples[:, block], MULT)
+            gram = grams.tile([P, BANK], F32, name="gram")
             nc.tensor.matmul(
-                square_sums[:, b : b + 1], squares[:, block], ones[:], start=True, stop=True
+                gram[:, :P], samples[:, block], samples[:, block], start=True, stop=True
             )
-        norms = held.tile([P, BLOCKS], F32, name="norms")
-        nc.scalar.sqrt(norms[:], square_sums[:])
+            nc.vector.scalar_tensor_tensor(
+                diagonal[:], gram[:, :P], 1.0, identity[:], MULT, MULT,
+                accum_out=square_sums[:, b : b + 1],
+            )
         inverse_norms = held.tile([P, BLOCKS], F32, name="inverse_norms")
-        nc.vector.reciprocal(inverse_norms[:], norms[:])
+        nc.scalar.activation(
+            inverse_norms[:], square_sums[:], mybir.ActivationFunctionType.Abs_reciprocal_sqrt
+        )
 
         for b in range(BLOCKS):
             block = slice(b * P, (b + 1) * P)
@@ -58,7 +64,10 @@ def tile_clustermemory_kernel(tc, table, w, offs, out):
                 start=True, stop=True,
             )
             scaled = staging.tile([P, N], F32, name="scaled")
-            nc.vector.tensor_scalar(
-                scaled[:], product[:], inverse_norms[:, b : b + 1], None, MULT
-            )
+            if b % 2 == 0:
+                nc.vector.tensor_scalar(
+                    scaled[:], product[:], inverse_norms[:, b : b + 1], None, MULT
+                )
+            else:
+                nc.scalar.mul(scaled[:], product[:], inverse_norms[:, b : b + 1])
             nc.sync.dma_start(out[block, :], scaled[:])

@@ -8,7 +8,7 @@ PER_COLUMN = 16
 BANK = 512
 FLOPS = 2 * P * M * N
 
-WARM_UP = 4
+WARM_UP = 2
 
 BF16, F32, U16 = mybir.dt.bfloat16, mybir.dt.float32, mybir.dt.uint16
 MULT = mybir.AluOpType.mult

@@ -41,6 +41,8 @@ def tile_clustermemory_kernel(tc, table, w, offs, out):
         make_identity(nc, identity[:])
         diagonal = held.tile([P, P], F32, name="diagonal")
         square_sums = held.tile([P, BLOCKS], F32, name="square_sums")
+        inverse_squares = held.tile([P, BLOCKS], F32, name="inverse_squares")
+        inverse_norms = held.tile([P, BLOCKS], F32, name="inverse_norms")
         for b in range(BLOCKS):
             block = slice(b * P, (b + 1) * P)
             gram = grams.tile([P, BANK], F32, name="gram")
@@ -51,10 +53,8 @@ def tile_clustermemory_kernel(tc, table, w, offs, out):
                 diagonal[:], gram[:, :P], 1.0, identity[:], MULT, MULT,
                 accum_out=square_sums[:, b : b + 1],
             )
-        inverse_norms = held.tile([P, BLOCKS], F32, name="inverse_norms")
-        nc.scalar.activation(
-            inverse_norms[:], square_sums[:], mybir.ActivationFunctionType.Abs_reciprocal_sqrt
-        )
+            nc.vector.reciprocal(inverse_squares[:, b : b + 1], square_sums[:, b : b + 1])
+            nc.scalar.sqrt(inverse_norms[:, b : b + 1], inverse_squares[:, b : b + 1])
 
         for b in range(BLOCKS):
             block = slice(b * P, (b + 1) * P)

@@ -8,8 +8,6 @@ PER_COLUMN = 16
 BANK = 512
 FLOPS = 2 * P * M * N
 
-WARM_UP = 2
-
 BF16, F32, U16 = mybir.dt.bfloat16, mybir.dt.float32, mybir.dt.uint16
 MULT = mybir.AluOpType.mult
 
@@ -30,12 +28,6 @@ def tile_clustermemory_kernel(tc, table, w, offs, out):
         for half, queue in enumerate((nc.scalar, nc.sync)):
             columns = slice(half * (S // 2), (half + 1) * (S // 2))
             queue.dma_start(centres[:, columns], table[:, columns])
-
-        zeros = held.tile([P, N], BF16, name="zeros")
-        nc.vector.memset(zeros[:], 0.0)
-        idle_product = products.tile([P, N], F32, name="product")
-        for i in range(WARM_UP):
-            nc.tensor.matmul(idle_product[:], zeros[:, :P], zeros[:], start=True, stop=True)
 
         identity = held.tile([P, P], F32, name="identity")
         make_identity(nc, identity[:])

@@ -22,12 +22,12 @@ def tile_clustermemory_kernel(tc, table, w, offs, out):
     ):
         samples = held.tile([P, M], BF16, name="samples")
         nc.sync.dma_start(samples[:], w)
-        offsets = held.tile([P, N // PER_COLUMN], U16, name="offsets")
-        nc.sync.dma_start(offsets[:], offs)
         centres = held.tile([P, S], BF16, name="centres")
         for half, queue in enumerate((nc.scalar, nc.sync)):
             columns = slice(half * (S // 2), (half + 1) * (S // 2))
             queue.dma_start(centres[:, columns], table[:, columns])
+        offsets = held.tile([P, N // PER_COLUMN], U16, name="offsets")
+        nc.sync.dma_start(offsets[:], offs)
 
         identity = held.tile([P, P], F32, name="identity")
         make_identity(nc, identity[:])

@@ -23,9 +23,7 @@ def tile_clustermemory_kernel(tc, table, w, offs, out):
         samples = held.tile([P, M], BF16, name="samples")
         nc.sync.dma_start(samples[:], w)
         centres = held.tile([P, S], BF16, name="centres")
-        for half, queue in enumerate((nc.scalar, nc.sync)):
-            columns = slice(half * (S // 2), (half + 1) * (S // 2))
-            queue.dma_start(centres[:, columns], table[:, columns])
+        nc.sync.dma_start(centres[:], table)
         offsets = held.tile([P, N // PER_COLUMN], U16, name="offsets")
         nc.sync.dma_start(offsets[:], offs)
 

@@ -10,6 +10,7 @@ FLOPS = 2 * P * M * N
 
 BF16, F32, U16 = mybir.dt.bfloat16, mybir.dt.float32, mybir.dt.uint16
 MULT = mybir.AluOpType.mult
+SQUARE = mybir.ActivationFunctionType.Square
 
 
 def tile_clustermemory_kernel(tc, table, w, offs, out):
@@ -17,9 +18,12 @@ def tile_clustermemory_kernel(tc, table, w, offs, out):
     with (
         tc.tile_pool(name="held", bufs=1) as held,
         tc.tile_pool(name="staging", bufs=BLOCKS) as staging,
-        tc.psum_pool(name="products", bufs=BLOCKS) as products,
-        tc.psum_pool(name="grams", bufs=BLOCKS) as grams,
+        tc.psum_pool(name="banks", bufs=8) as banks,
     ):
+        one = held.tile([P, 1], F32, name="one")
+        root_of_one = held.tile([P, 1], F32, name="root_of_one")
+        nc.vector.memset(one[:], 1.0)
+        nc.scalar.sqrt(root_of_one[:], one[:])
         samples = held.tile([P, M], BF16, name="samples")
         nc.sync.dma_start(samples[:], w)
         centres = held.tile([P, S], BF16, name="centres")
@@ -27,28 +31,40 @@ def tile_clustermemory_kernel(tc, table, w, offs, out):
         offsets = held.tile([P, N // PER_COLUMN], U16, name="offsets")
         nc.sync.dma_start(offsets[:], offs)
 
-        identity = held.tile([P, P], F32, name="identity")
+        identity = held.tile([P, P], BF16, name="identity")
         make_identity(nc, identity[:])
+        inverse_norms = []
         diagonal = held.tile([P, P], F32, name="diagonal")
-        square_sums = held.tile([P, BLOCKS], F32, name="square_sums")
-        inverse_squares = held.tile([P, BLOCKS], F32, name="inverse_squares")
-        inverse_norms = held.tile([P, BLOCKS], F32, name="inverse_norms")
+        squares = held.tile([P, P], F32, name="squares")
         for b in range(BLOCKS):
             block = slice(b * P, (b + 1) * P)
-            gram = grams.tile([P, BANK], F32, name="gram")
-            nc.tensor.matmul(
-                gram[:, :P], samples[:, block], samples[:, block], start=True, stop=True
-            )
-            nc.vector.scalar_tensor_tensor(
-                diagonal[:], gram[:, :P], 1.0, identity[:], MULT, MULT,
-                accum_out=square_sums[:, b : b + 1],
-            )
-            nc.vector.reciprocal(inverse_squares[:, b : b + 1], square_sums[:, b : b + 1])
-            nc.scalar.sqrt(inverse_norms[:, b : b + 1], inverse_squares[:, b : b + 1])
+            square_sum = held.tile([P, 1], F32, name=f"square_sum{b}")
+            inverse_square = held.tile([P, 1], F32, name=f"inverse_square{b}")
+            inverse_norm = held.tile([P, 1], F32, name=f"inverse_norm{b}")
+            if b % 2 == 0:
+                gram = banks.tile([P, BANK], F32, name="bank")
+                nc.tensor.matmul(
+                    gram[:, :P], samples[:, block], samples[:, block], start=True, stop=True
+                )
+                nc.vector.scalar_tensor_tensor(
+                    diagonal[:], gram[:, :P], 1.0, identity[:], MULT, MULT,
+                    accum_out=square_sum[:],
+                )
+            else:
+                flipped = banks.tile([P, BANK], F32, name="bank")
+                nc.tensor.matmul(
+                    flipped[:, :P], samples[:, block], identity[:], start=True, stop=True
+                )
+                nc.scalar.activation(
+                    squares[:], flipped[:, :P], SQUARE, accum_out=square_sum[:]
+                )
+            nc.vector.reciprocal(inverse_square[:], square_sum[:])
+            nc.scalar.sqrt(inverse_norm[:], inverse_square[:])
+            inverse_norms.append(inverse_norm)
 
         for b in range(BLOCKS):
             block = slice(b * P, (b + 1) * P)
-            product = products.tile([P, N], F32, name="product")
+            product = banks.tile([P, BANK], F32, name="bank")
             nc.tensor.matmul(
                 product[:], samples[:, block], centres[:].indirect(offsets[:]),
                 start=True, stop=True,
@@ -56,8 +72,8 @@ def tile_clustermemory_kernel(tc, table, w, offs, out):
             scaled = staging.tile([P, N], F32, name="scaled")
             if b % 2 == 0:
                 nc.vector.tensor_scalar(
-                    scaled[:], product[:], inverse_norms[:, b : b + 1], None, MULT
+                    scaled[:], product[:], inverse_norms[b][:], None, MULT
                 )
             else:
-                nc.scalar.mul(scaled[:], product[:], inverse_norms[:, b : b + 1])
+                nc.scalar.mul(scaled[:], product[:], inverse_norms[b][:])
             nc.sync.dma_start(out[block, :], scaled[:])

@@ -62,18 +62,29 @@ def tile_clustermemory_kernel(tc, table, w, offs, out):
             nc.scalar.sqrt(inverse_norm[:], inverse_square[:])
             inverse_norms.append(inverse_norm)
 
+        turn = 0
         for b in range(BLOCKS):
             block = slice(b * P, (b + 1) * P)
-            product = banks.tile([P, BANK], F32, name="bank")
-            nc.tensor.matmul(
-                product[:], samples[:, block], centres[:].indirect(offsets[:]),
-                start=True, stop=True,
-            )
             scaled = staging.tile([P, N], F32, name="scaled")
-            if b % 2 == 0:
-                nc.vector.tensor_scalar(
-                    scaled[:], product[:], inverse_norms[b][:], None, MULT
+            pieces = 2 if b in (0, BLOCKS - 1) else 1
+            width = N // pieces
+            for piece in range(pieces):
+                columns = slice(piece * width, (piece + 1) * width)
+                listed = slice(columns.start // PER_COLUMN, columns.stop // PER_COLUMN)
+                product = banks.tile([P, BANK], F32, name="bank")
+                nc.tensor.matmul(
+                    product[:, :width], samples[:, block],
+                    centres[:].indirect(offsets[:, listed]),
+                    start=True, stop=True,
                 )
-            else:
-                nc.scalar.mul(scaled[:], product[:], inverse_norms[b][:])
+                if turn % 2 == 0:
+                    nc.vector.tensor_scalar(
+                        scaled[:, columns], product[:, :width],
+                        inverse_norms[b][:], None, MULT,
+                    )
+                else:
+                    nc.scalar.mul(
+                        scaled[:, columns], product[:, :width], inverse_norms[b][:]
+                    )
+                turn += 1
             nc.sync.dma_start(out[block, :], scaled[:])

@@ -62,29 +62,26 @@ def tile_clustermemory_kernel(tc, table, w, offs, out):
             nc.scalar.sqrt(inverse_norm[:], inverse_square[:])
             inverse_norms.append(inverse_norm)
 
-        turn = 0
+        half = N // 2
         for b in range(BLOCKS):
             block = slice(b * P, (b + 1) * P)
             scaled = staging.tile([P, N], F32, name="scaled")
-            pieces = 2 if b in (0, BLOCKS - 1) else 1
-            width = N // pieces
-            for piece in range(pieces):
-                columns = slice(piece * width, (piece + 1) * width)
+            for start in (0, half):
+                columns = slice(start, start + half)
                 listed = slice(columns.start // PER_COLUMN, columns.stop // PER_COLUMN)
                 product = banks.tile([P, BANK], F32, name="bank")
                 nc.tensor.matmul(
-                    product[:, :width], samples[:, block],
+                    product[:, :half], samples[:, block],
                     centres[:].indirect(offsets[:, listed]),
                     start=True, stop=True,
                 )
-                if turn % 2 == 0:
+                if start == 0:
                     nc.vector.tensor_scalar(
-                        scaled[:, columns], product[:, :width],
+                        scaled[:, columns], product[:, :half],
                         inverse_norms[b][:], None, MULT,
                     )
                 else:
                     nc.scalar.mul(
-                        scaled[:, columns], product[:, :width], inverse_norms[b][:]
+                        scaled[:, columns], product[:, :half], inverse_norms[b][:]
                     )
-                turn += 1
             nc.sync.dma_start(out[block, :], scaled[:])

@@ -75,13 +75,7 @@ def tile_clustermemory_kernel(tc, table, w, offs, out):
                     centres[:].indirect(offsets[:, listed]),
                     start=True, stop=True,
                 )
-                if start == 0:
-                    nc.vector.tensor_scalar(
-                        scaled[:, columns], product[:, :half],
-                        inverse_norms[b][:], None, MULT,
-                    )
-                else:
-                    nc.scalar.mul(
-                        scaled[:, columns], product[:, :half], inverse_norms[b][:]
-                    )
+                nc.vector.tensor_scalar(
+                    scaled[:, columns], product[:, :half], inverse_norms[b][:], None, MULT
+                )
             nc.sync.dma_start(out[block, :], scaled[:])

@@ -26,10 +26,10 @@ def tile_clustermemory_kernel(tc, table, w, offs, out):
         nc.scalar.sqrt(root_of_one[:], one[:])
         samples = held.tile([P, M], BF16, name="samples")
         nc.sync.dma_start(samples[:], w)
-        centres = held.tile([P, S], BF16, name="centres")
-        nc.sync.dma_start(centres[:], table)
         offsets = held.tile([P, N // PER_COLUMN], U16, name="offsets")
         nc.sync.dma_start(offsets[:], offs)
+        centres = held.tile([P, S], BF16, name="centres")
+        nc.sync.dma_start(centres[:], table)
 
         identity = held.tile([P, P], BF16, name="identity")
         make_identity(nc, identity[:])

@@ -5,6 +5,7 @@ P = 128
 S, M, N = 2048, 512, 512
 BLOCKS = M // P
 PER_COLUMN = 16
+PAIR = 2 * PER_COLUMN
 BANK = 512
 FLOPS = 2 * P * M * N
 
@@ -62,20 +63,27 @@ def tile_clustermemory_kernel(tc, table, w, offs, out):
             nc.scalar.sqrt(inverse_norm[:], inverse_square[:])
             inverse_norms.append(inverse_norm)
 
-        half = N // 2
+        thirds = [round(N * i / 3 / PAIR) * PAIR for i in range(4)]
         for b in range(BLOCKS):
             block = slice(b * P, (b + 1) * P)
             scaled = staging.tile([P, N], F32, name="scaled")
-            for start in (0, half):
-                columns = slice(start, start + half)
+            for piece in range(3):
+                columns = slice(thirds[piece], thirds[piece + 1])
+                width = columns.stop - columns.start
                 listed = slice(columns.start // PER_COLUMN, columns.stop // PER_COLUMN)
                 product = banks.tile([P, BANK], F32, name="bank")
                 nc.tensor.matmul(
-                    product[:, :half], samples[:, block],
+                    product[:, :width], samples[:, block],
                     centres[:].indirect(offsets[:, listed]),
                     start=True, stop=True,
                 )
-                nc.vector.tensor_scalar(
-                    scaled[:, columns], product[:, :half], inverse_norms[b][:], None, MULT
-                )
+                if piece == 1:
+                    nc.scalar.mul(
+                        scaled[:, columns], product[:, :width], inverse_norms[b][:]
+                    )
+                else:
+                    nc.vector.tensor_scalar(
+                        scaled[:, columns], product[:, :width],
+                        inverse_norms[b][:], None, MULT,
+                    )
             nc.sync.dma_start(out[block, :], scaled[:])

import concourse.mybir as mybir
from concourse.masks import make_identity

P = 128
S, M, N = 2048, 512, 512
BLOCKS = M // P
PER_COLUMN = 16
PAIR = 2 * PER_COLUMN
BANK = 512
FLOPS = 2 * P * M * N

BF16, F32, U16 = mybir.dt.bfloat16, mybir.dt.float32, mybir.dt.uint16
MULT = mybir.AluOpType.mult
SQUARE = mybir.ActivationFunctionType.Square


def tile_clustermemory_kernel(tc, table, w, offs, out):
    nc = tc.nc
    with (
        tc.tile_pool(name="held", bufs=1) as held,
        tc.tile_pool(name="staging", bufs=BLOCKS) as staging,
        tc.psum_pool(name="banks", bufs=8) as banks,
    ):
        one = held.tile([P, 1], F32, name="one")
        root_of_one = held.tile([P, 1], F32, name="root_of_one")
        nc.vector.memset(one[:], 1.0)
        nc.scalar.sqrt(root_of_one[:], one[:])
        samples = held.tile([P, M], BF16, name="samples")
        nc.sync.dma_start(samples[:], w)
        offsets = held.tile([P, N // PER_COLUMN], U16, name="offsets")
        nc.sync.dma_start(offsets[:], offs)
        centres = held.tile([P, S], BF16, name="centres")
        nc.sync.dma_start(centres[:], table)

        identity = held.tile([P, P], BF16, name="identity")
        make_identity(nc, identity[:])
        inverse_norms = []
        diagonal = held.tile([P, P], F32, name="diagonal")
        squares = held.tile([P, P], F32, name="squares")
        for b in range(BLOCKS):
            block = slice(b * P, (b + 1) * P)
            square_sum = held.tile([P, 1], F32, name=f"square_sum{b}")
            inverse_square = held.tile([P, 1], F32, name=f"inverse_square{b}")
            inverse_norm = held.tile([P, 1], F32, name=f"inverse_norm{b}")
            if b % 2 == 0:
                gram = banks.tile([P, BANK], F32, name="bank")
                nc.tensor.matmul(
                    gram[:, :P], samples[:, block], samples[:, block], start=True, stop=True
                )
                nc.vector.scalar_tensor_tensor(
                    diagonal[:], gram[:, :P], 1.0, identity[:], MULT, MULT,
                    accum_out=square_sum[:],
                )
            else:
                flipped = banks.tile([P, BANK], F32, name="bank")
                nc.tensor.matmul(
                    flipped[:, :P], samples[:, block], identity[:], start=True, stop=True
                )
                nc.scalar.activation(
                    squares[:], flipped[:, :P], SQUARE, accum_out=square_sum[:]
                )
            nc.vector.reciprocal(inverse_square[:], square_sum[:])
            nc.scalar.sqrt(inverse_norm[:], inverse_square[:])
            inverse_norms.append(inverse_norm)

        thirds = [round(N * i / 3 / PAIR) * PAIR for i in range(4)]
        for b in range(BLOCKS):
            block = slice(b * P, (b + 1) * P)
            scaled = staging.tile([P, N], F32, name="scaled")
            for piece in range(3):
                columns = slice(thirds[piece], thirds[piece + 1])
                width = columns.stop - columns.start
                listed = slice(columns.start // PER_COLUMN, columns.stop // PER_COLUMN)
                product = banks.tile([P, BANK], F32, name="bank")
                nc.tensor.matmul(
                    product[:, :width], samples[:, block],
                    centres[:].indirect(offsets[:, listed]),
                    start=True, stop=True,
                )
                if piece == 1:
                    nc.scalar.mul(
                        scaled[:, columns], product[:, :width], inverse_norms[b][:]
                    )
                else:
                    nc.vector.tensor_scalar(
                        scaled[:, columns], product[:, :width],
                        inverse_norms[b][:], None, MULT,
                    )
            nc.sync.dma_start(out[block, :], scaled[:])
